import numpy as np
import ml_dtypes

BF16 = ml_dtypes.bfloat16


def bf(x):
    return np.asarray(x, np.float32).astype(BF16)


def f32(x):
    return np.asarray(x, np.float32)


def f64(x):
    return np.asarray(x).astype(np.float64)


def striped(idx):
    return np.tile(idx.reshape(-1, 16).T, (8, 1))


S, D, M, N, DH = 1024, 128, 256, 256, 64
THETA = 10000.0


def rope_tables():
    inv = np.float32(1.0) / np.float32(THETA) ** (np.arange(0, DH, 2).astype(np.float32) / np.float32(DH))
    ang = np.arange(N).astype(np.float32)[None, :] * np.concatenate([inv, inv])[:, None]
    ang = np.tile(ang, (M // DH, 1))
    return f32(np.cos(f64(ang))), f32(np.sin(f64(ang)))


def rot_half(v):
    r = v.reshape(M // DH, 2, DH // 2, -1)
    return np.concatenate([-r[:, 1:2], r[:, 0:1]], axis=1).reshape(v.shape)


def setup_inputs():
    cos_t, sin_t = rope_tables()
    return {"table": bf(np.random.standard_normal((D, S))), "w": bf(np.random.standard_normal((D, M)) / np.sqrt(D)), "b": f32(0.1 * np.random.standard_normal((M, 1))), "cos_t": cos_t, "sin_t": sin_t, "offs": striped(np.random.permutation(np.tile(np.arange(S), 2))[:N])}


def reference(table, w, b, cos_t, sin_t, offs):
    idx = offs[:16].T.reshape(-1)
    p = f64(w).T @ f64(table)[:, idx] + f64(b)
    return p * f64(cos_t) + rot_half(p) * f64(sin_t)

@@ -1,0 +1,66 @@
+import concourse.mybir as mybir
+
+P = 128
+WORDS = 1024
+FEATS = 256
+TOKENS = 256
+HALF = 32
+BLOCKS = FEATS // P
+FLOPS = 2 * P * FEATS * TOKENS
+
+BF16, F32, U16 = mybir.dt.bfloat16, mybir.dt.float32, mybir.dt.uint16
+ADD, MULT = mybir.AluOpType.add, mybir.AluOpType.mult
+
+
+def tile_molformer_kernel(tc, table, w, b, cos_t, sin_t, offs, out):
+    nc = tc.nc
+    with (
+        tc.tile_pool(name="held", bufs=1) as held,
+        tc.tile_pool(name="work", bufs=2) as work,
+        tc.psum_pool(name="psum", bufs=1) as psum,
+    ):
+        offsets = held.tile([P, TOKENS // 16], U16, name="offsets")
+        nc.sync.dma_start(offsets[:], offs)
+        words = held.tile([P, WORDS], BF16, name="words")
+        nc.sync.dma_start(words[:], table)
+        w_plain = held.tile([P, FEATS], BF16, name="w_plain")
+        nc.scalar.dma_start(w_plain[:], w)
+        cos_sb = [held.tile([P, TOKENS], F32, name=f"cos{k}") for k in range(BLOCKS)]
+        sin_sb = [held.tile([P, TOKENS], F32, name=f"sin{k}") for k in range(BLOCKS)]
+        for k in range(BLOCKS):
+            nc.scalar.dma_start(cos_sb[k][:], cos_t[k * P : (k + 1) * P, :])
+            nc.sync.dma_start(sin_sb[k][:], sin_t[k * P : (k + 1) * P, :])
+
+        w_turned = held.tile([P, FEATS], BF16, name="w_turned")
+        to = w_turned[:].rearrange("p (h t q) -> p h t q", t=2, q=HALF)
+        frm = w_plain[:].rearrange("p (h t q) -> p h t q", t=2, q=HALF)
+        nc.vector.tensor_scalar_mul(to[:, :, 0, :], frm[:, :, 1, :], -1.0)
+        nc.vector.tensor_copy(to[:, :, 1, :], frm[:, :, 0, :])
+
+        b_cols = b.rearrange("(k p) o -> p (k o)", p=P)
+        b_plain = held.tile([P, BLOCKS], F32, name="b_plain")
+        b_turned = held.tile([P, BLOCKS], F32, name="b_turned")
+        with nc.allow_non_contiguous_dma(reason="a bias of 256 values, one value to a partition"):
+            nc.gpsimd.dma_start(b_plain[:], b_cols)
+            for first in range(0, P, 2 * HALF):
+                second = first + HALF
+                nc.gpsimd.dma_start(b_turned[first : first + HALF, :], b_cols[second : second + HALF, :])
+                nc.gpsimd.dma_start(b_turned[second : second + HALF, :], b_cols[first : first + HALF, :])
+        for first in range(0, P, 2 * HALF):
+            nc.gpsimd.tensor_scalar_mul(b_turned[first : first + HALF, :], b_turned[first : first + HALF, :], -1.0)
+
+        for k in range(BLOCKS):
+            block = slice(k * P, (k + 1) * P)
+            p_ps = psum.tile([P, TOKENS], F32, name=f"p_ps{k}")
+            nc.tensor.matmul(p_ps[:], w_plain[:, block], words[:].indirect(offsets[:]))
+            r_ps = psum.tile([P, TOKENS], F32, name=f"r_ps{k}")
+            nc.tensor.matmul(r_ps[:], w_turned[:, block], words[:].indirect(offsets[:]))
+
+            by_cos = work.tile([P, TOKENS], F32, name="by_cos")
+            nc.vector.scalar_tensor_tensor(by_cos[:], p_ps[:], b_plain[:, k : k + 1], cos_sb[k][:], ADD, MULT)
+            by_sin = work.tile([P, TOKENS], F32, name="by_sin")
+            nc.vector.scalar_tensor_tensor(by_sin[:], r_ps[:], b_turned[:, k : k + 1], sin_sb[k][:], ADD, MULT)
+            turned = work.tile([P, TOKENS], F32, name="turned")
+            nc.vector.tensor_add(turned[:], by_cos[:], by_sin[:])
+            queue = nc.sync if k == 0 else nc.scalar
+            queue.dma_start(out[block, :], turned[:])

@@ -1,4 +1,5 @@
 import concourse.mybir as mybir
+from concourse.masks import make_identity
 
 P = 128
 WORDS = 1024
@@ -12,11 +13,17 @@ BF16, F32, U16 = mybir.dt.bfloat16, mybir.dt.float32, mybir.dt.uint16
 ADD, MULT = mybir.AluOpType.add, mybir.AluOpType.mult
 
 
+def rotate_half_columns(nc, dst, src):
+    d = dst.rearrange("r (h t q) -> r h t q", t=2, q=HALF)
+    s = src.rearrange("r (h t q) -> r h t q", t=2, q=HALF)
+    nc.vector.tensor_scalar_mul(d[:, :, 0, :], s[:, :, 1, :], -1.0)
+    nc.vector.tensor_copy(d[:, :, 1, :], s[:, :, 0, :])
+
+
 def tile_molformer_kernel(tc, table, w, b, cos_t, sin_t, offs, out):
     nc = tc.nc
     with (
         tc.tile_pool(name="held", bufs=1) as held,
-        tc.tile_pool(name="work", bufs=2) as work,
         tc.psum_pool(name="psum", bufs=1) as psum,
     ):
         offsets = held.tile([P, TOKENS // 16], U16, name="offsets")
@@ -25,42 +32,43 @@ def tile_molformer_kernel(tc, table, w, b, cos_t, sin_t, offs, out):
         nc.sync.dma_start(words[:], table)
         w_plain = held.tile([P, FEATS], BF16, name="w_plain")
         nc.scalar.dma_start(w_plain[:], w)
+        b_plain = held.tile([BLOCKS, P], F32, name="b_plain")
+        nc.scalar.dma_start(b_plain[:], b.rearrange("(k m) o -> k (m o)", k=BLOCKS))
         cos_sb = [held.tile([P, TOKENS], F32, name=f"cos{k}") for k in range(BLOCKS)]
         sin_sb = [held.tile([P, TOKENS], F32, name=f"sin{k}") for k in range(BLOCKS)]
         for k in range(BLOCKS):
-            nc.scalar.dma_start(cos_sb[k][:], cos_t[k * P : (k + 1) * P, :])
-            nc.sync.dma_start(sin_sb[k][:], sin_t[k * P : (k + 1) * P, :])
+            nc.sync.dma_start(cos_sb[k][:], cos_t[k * P : (k + 1) * P, :])
+            nc.scalar.dma_start(sin_sb[k][:], sin_t[k * P : (k + 1) * P, :])
 
+        b_turned = held.tile([BLOCKS, P], F32, name="b_turned")
+        rotate_half_columns(nc, b_turned[:], b_plain[:])
         w_turned = held.tile([P, FEATS], BF16, name="w_turned")
-        to = w_turned[:].rearrange("p (h t q) -> p h t q", t=2, q=HALF)
-        frm = w_plain[:].rearrange("p (h t q) -> p h t q", t=2, q=HALF)
-        nc.vector.tensor_scalar_mul(to[:, :, 0, :], frm[:, :, 1, :], -1.0)
-        nc.vector.tensor_copy(to[:, :, 1, :], frm[:, :, 0, :])
+        rotate_half_columns(nc, w_turned[:], w_plain[:])
 
-        b_cols = b.rearrange("(k p) o -> p (k o)", p=P)
-        b_plain = held.tile([P, BLOCKS], F32, name="b_plain")
-        b_turned = held.tile([P, BLOCKS], F32, name="b_turned")
-        with nc.allow_non_contiguous_dma(reason="a bias of 256 values, one value to a partition"):
-            nc.gpsimd.dma_start(b_plain[:], b_cols)
-            for first in range(0, P, 2 * HALF):
-                second = first + HALF
-                nc.gpsimd.dma_start(b_turned[first : first + HALF, :], b_cols[second : second + HALF, :])
-                nc.gpsimd.dma_start(b_turned[second : second + HALF, :], b_cols[first : first + HALF, :])
-        for first in range(0, P, 2 * HALF):
-            nc.gpsimd.tensor_scalar_mul(b_turned[first : first + HALF, :], b_turned[first : first + HALF, :], -1.0)
+        ident = held.tile([BLOCKS, BLOCKS], F32, name="ident")
+        make_identity(nc, ident[:])
+        bias_ps = psum.tile([P, 2 * BLOCKS], F32, name="bias_ps")
+        nc.tensor.matmul(bias_ps[:, 0:BLOCKS], b_plain[:], ident[:])
+        nc.tensor.matmul(bias_ps[:, BLOCKS : 2 * BLOCKS], b_turned[:], ident[:])
+        bias = held.tile([P, 2 * BLOCKS], F32, name="bias")
+        nc.vector.tensor_copy(bias[:], bias_ps[:])
 
+        p_ps = [psum.tile([P, TOKENS], F32, name=f"p_ps{k}") for k in range(BLOCKS)]
+        r_ps = [psum.tile([P, TOKENS], F32, name=f"r_ps{k}") for k in range(BLOCKS)]
         for k in range(BLOCKS):
             block = slice(k * P, (k + 1) * P)
-            p_ps = psum.tile([P, TOKENS], F32, name=f"p_ps{k}")
-            nc.tensor.matmul(p_ps[:], w_plain[:, block], words[:].indirect(offsets[:]))
-            r_ps = psum.tile([P, TOKENS], F32, name=f"r_ps{k}")
-            nc.tensor.matmul(r_ps[:], w_turned[:, block], words[:].indirect(offsets[:]))
+            nc.tensor.matmul(p_ps[k][:], w_plain[:, block], words[:].indirect(offsets[:]))
+            nc.tensor.matmul(r_ps[k][:], w_turned[:, block], words[:].indirect(offsets[:]))
 
-            by_cos = work.tile([P, TOKENS], F32, name="by_cos")
-            nc.vector.scalar_tensor_tensor(by_cos[:], p_ps[:], b_plain[:, k : k + 1], cos_sb[k][:], ADD, MULT)
-            by_sin = work.tile([P, TOKENS], F32, name="by_sin")
-            nc.vector.scalar_tensor_tensor(by_sin[:], r_ps[:], b_turned[:, k : k + 1], sin_sb[k][:], ADD, MULT)
-            turned = work.tile([P, TOKENS], F32, name="turned")
-            nc.vector.tensor_add(turned[:], by_cos[:], by_sin[:])
-            queue = nc.sync if k == 0 else nc.scalar
-            queue.dma_start(out[block, :], turned[:])
+        by_cos = [held.tile([P, TOKENS], F32, name=f"by_cos{k}") for k in range(BLOCKS)]
+        by_sin = [held.tile([P, TOKENS], F32, name=f"by_sin{k}") for k in range(BLOCKS)]
+        for k in range(BLOCKS):
+            nc.vector.scalar_tensor_tensor(by_cos[k][:], p_ps[k][:], bias[:, k : k + 1], cos_sb[k][:], ADD, MULT)
+            nc.vector.scalar_tensor_tensor(
+                by_sin[k][:], r_ps[k][:], bias[:, BLOCKS + k : BLOCKS + k + 1], sin_sb[k][:], ADD, MULT
+            )
+        for k in range(BLOCKS):
+            turned = held.tile([P, TOKENS], F32, name=f"turned{k}")
+            nc.vector.tensor_add(turned[:], by_cos[k][:], by_sin[k][:])
+            queue = nc.sync if k % 2 == 0 else nc.scalar
+            queue.dma_start(out[k * P : (k + 1) * P, :], turned[:])

@@ -1,5 +1,4 @@
 import concourse.mybir as mybir
-from concourse.masks import make_identity
 
 P = 128
 WORDS = 1024
@@ -26,30 +25,31 @@ def tile_molformer_kernel(tc, table, w, b, cos_t, sin_t, offs, out):
         tc.tile_pool(name="held", bufs=1) as held,
         tc.psum_pool(name="psum", bufs=1) as psum,
     ):
+        b_plain = held.tile([1, FEATS], F32, name="b_plain")
+        nc.sync.dma_start(b_plain[:], b.rearrange("m o -> o m"))
         offsets = held.tile([P, TOKENS // 16], U16, name="offsets")
         nc.sync.dma_start(offsets[:], offs)
-        words = held.tile([P, WORDS], BF16, name="words")
-        nc.sync.dma_start(words[:], table)
         w_plain = held.tile([P, FEATS], BF16, name="w_plain")
         nc.scalar.dma_start(w_plain[:], w)
-        b_plain = held.tile([BLOCKS, P], F32, name="b_plain")
-        nc.scalar.dma_start(b_plain[:], b.rearrange("(k m) o -> k (m o)", k=BLOCKS))
+        words = held.tile([P, WORDS], BF16, name="words")
+        nc.sync.dma_start(words[:], table)
         cos_sb = [held.tile([P, TOKENS], F32, name=f"cos{k}") for k in range(BLOCKS)]
         sin_sb = [held.tile([P, TOKENS], F32, name=f"sin{k}") for k in range(BLOCKS)]
         for k in range(BLOCKS):
-            nc.sync.dma_start(cos_sb[k][:], cos_t[k * P : (k + 1) * P, :])
-            nc.scalar.dma_start(sin_sb[k][:], sin_t[k * P : (k + 1) * P, :])
+            nc.scalar.dma_start(cos_sb[k][:], cos_t[k * P : (k + 1) * P, :])
+            nc.sync.dma_start(sin_sb[k][:], sin_t[k * P : (k + 1) * P, :])
 
-        b_turned = held.tile([BLOCKS, P], F32, name="b_turned")
+        b_turned = held.tile([1, FEATS], F32, name="b_turned")
         rotate_half_columns(nc, b_turned[:], b_plain[:])
         w_turned = held.tile([P, FEATS], BF16, name="w_turned")
         rotate_half_columns(nc, w_turned[:], w_plain[:])
 
-        ident = held.tile([BLOCKS, BLOCKS], F32, name="ident")
-        make_identity(nc, ident[:])
+        one = held.tile([1, 1], F32, name="one")
+        nc.vector.memset(one[:], 1.0)
         bias_ps = psum.tile([P, 2 * BLOCKS], F32, name="bias_ps")
-        nc.tensor.matmul(bias_ps[:, 0:BLOCKS], b_plain[:], ident[:])
-        nc.tensor.matmul(bias_ps[:, BLOCKS : 2 * BLOCKS], b_turned[:], ident[:])
+        for i, row in enumerate((b_plain, b_turned)):
+            for k in range(BLOCKS):
+                nc.tensor.matmul(bias_ps[:, i * BLOCKS + k : i * BLOCKS + k + 1], row[:, k * P : (k + 1) * P], one[:])
         bias = held.tile([P, 2 * BLOCKS], F32, name="bias")
         nc.vector.tensor_copy(bias[:], bias_ps[:])
 

@@ -6,6 +6,7 @@ FEATS = 256
 TOKENS = 256
 HALF = 32
 BLOCKS = FEATS // P
+WARM_UP = 8
 FLOPS = 2 * P * FEATS * TOKENS
 
 BF16, F32, U16 = mybir.dt.bfloat16, mybir.dt.float32, mybir.dt.uint16
@@ -38,6 +39,12 @@ def tile_molformer_kernel(tc, table, w, b, cos_t, sin_t, offs, out):
         for k in range(BLOCKS):
             nc.scalar.dma_start(cos_sb[k][:], cos_t[k * P : (k + 1) * P, :])
             nc.sync.dma_start(sin_sb[k][:], sin_t[k * P : (k + 1) * P, :])
+
+        zeros = held.tile([P, TOKENS], BF16, name="zeros")
+        nc.vector.memset(zeros[:], 0.0)
+        warm_ps = psum.tile([P, TOKENS], F32, name="warm_ps")
+        for i in range(WARM_UP):
+            nc.tensor.matmul(warm_ps[:], zeros[:, 0:P], zeros[:])
 
         b_turned = held.tile([1, FEATS], F32, name="b_turned")
         rotate_half_columns(nc, b_turned[:], b_plain[:])

@@ -6,18 +6,10 @@ FEATS = 256
 TOKENS = 256
 HALF = 32
 BLOCKS = FEATS // P
-WARM_UP = 8
 FLOPS = 2 * P * FEATS * TOKENS
 
 BF16, F32, U16 = mybir.dt.bfloat16, mybir.dt.float32, mybir.dt.uint16
 ADD, MULT = mybir.AluOpType.add, mybir.AluOpType.mult
-
-
-def rotate_half_columns(nc, dst, src):
-    d = dst.rearrange("r (h t q) -> r h t q", t=2, q=HALF)
-    s = src.rearrange("r (h t q) -> r h t q", t=2, q=HALF)
-    nc.vector.tensor_scalar_mul(d[:, :, 0, :], s[:, :, 1, :], -1.0)
-    nc.vector.tensor_copy(d[:, :, 1, :], s[:, :, 0, :])
 
 
 def tile_molformer_kernel(tc, table, w, b, cos_t, sin_t, offs, out):
@@ -26,39 +18,36 @@ def tile_molformer_kernel(tc, table, w, b, cos_t, sin_t, offs, out):
         tc.tile_pool(name="held", bufs=1) as held,
         tc.psum_pool(name="psum", bufs=1) as psum,
     ):
-        b_plain = held.tile([1, FEATS], F32, name="b_plain")
-        nc.sync.dma_start(b_plain[:], b.rearrange("m o -> o m"))
         offsets = held.tile([P, TOKENS // 16], U16, name="offsets")
         nc.sync.dma_start(offsets[:], offs)
         w_plain = held.tile([P, FEATS], BF16, name="w_plain")
         nc.scalar.dma_start(w_plain[:], w)
         words = held.tile([P, WORDS], BF16, name="words")
         nc.sync.dma_start(words[:], table)
+
+        b_cols = b.rearrange("(k p) o -> p (k o)", p=P)
+        b_plain = held.tile([P, BLOCKS], F32, name="b_plain")
+        b_turned = held.tile([P, BLOCKS], F32, name="b_turned")
+        with nc.allow_non_contiguous_dma(reason="a bias of 256 values, one value to a partition"):
+            nc.scalar.dma_start(b_plain[:], b_cols)
+            for first in range(0, P, 2 * HALF):
+                second = first + HALF
+                nc.sync.dma_start(b_turned[first : first + HALF, :], b_cols[second : second + HALF, :])
+                nc.scalar.dma_start(b_turned[second : second + HALF, :], b_cols[first : first + HALF, :])
+
         cos_sb = [held.tile([P, TOKENS], F32, name=f"cos{k}") for k in range(BLOCKS)]
         sin_sb = [held.tile([P, TOKENS], F32, name=f"sin{k}") for k in range(BLOCKS)]
         for k in range(BLOCKS):
             nc.scalar.dma_start(cos_sb[k][:], cos_t[k * P : (k + 1) * P, :])
             nc.sync.dma_start(sin_sb[k][:], sin_t[k * P : (k + 1) * P, :])
 
-        zeros = held.tile([P, TOKENS], BF16, name="zeros")
-        nc.vector.memset(zeros[:], 0.0)
-        warm_ps = psum.tile([P, TOKENS], F32, name="warm_ps")
-        for i in range(WARM_UP):
-            nc.tensor.matmul(warm_ps[:], zeros[:, 0:P], zeros[:])
-
-        b_turned = held.tile([1, FEATS], F32, name="b_turned")
-        rotate_half_columns(nc, b_turned[:], b_plain[:])
         w_turned = held.tile([P, FEATS], BF16, name="w_turned")
-        rotate_half_columns(nc, w_turned[:], w_plain[:])
-
-        one = held.tile([1, 1], F32, name="one")
-        nc.vector.memset(one[:], 1.0)
-        bias_ps = psum.tile([P, 2 * BLOCKS], F32, name="bias_ps")
-        for i, row in enumerate((b_plain, b_turned)):
-            for k in range(BLOCKS):
-                nc.tensor.matmul(bias_ps[:, i * BLOCKS + k : i * BLOCKS + k + 1], row[:, k * P : (k + 1) * P], one[:])
-        bias = held.tile([P, 2 * BLOCKS], F32, name="bias")
-        nc.vector.tensor_copy(bias[:], bias_ps[:])
+        to = w_turned[:].rearrange("d (h t q) -> d h t q", t=2, q=HALF)
+        frm = w_plain[:].rearrange("d (h t q) -> d h t q", t=2, q=HALF)
+        nc.vector.tensor_scalar_mul(to[:, :, 0, :], frm[:, :, 1, :], -1.0)
+        nc.vector.tensor_copy(to[:, :, 1, :], frm[:, :, 0, :])
+        for first in range(0, P, 2 * HALF):
+            nc.gpsimd.tensor_scalar_mul(b_turned[first : first + HALF, :], b_turned[first : first + HALF, :], -1.0)
 
         p_ps = [psum.tile([P, TOKENS], F32, name=f"p_ps{k}") for k in range(BLOCKS)]
         r_ps = [psum.tile([P, TOKENS], F32, name=f"r_ps{k}") for k in range(BLOCKS)]
@@ -70,10 +59,8 @@ def tile_molformer_kernel(tc, table, w, b, cos_t, sin_t, offs, out):
         by_cos = [held.tile([P, TOKENS], F32, name=f"by_cos{k}") for k in range(BLOCKS)]
         by_sin = [held.tile([P, TOKENS], F32, name=f"by_sin{k}") for k in range(BLOCKS)]
         for k in range(BLOCKS):
-            nc.vector.scalar_tensor_tensor(by_cos[k][:], p_ps[k][:], bias[:, k : k + 1], cos_sb[k][:], ADD, MULT)
-            nc.vector.scalar_tensor_tensor(
-                by_sin[k][:], r_ps[k][:], bias[:, BLOCKS + k : BLOCKS + k + 1], sin_sb[k][:], ADD, MULT
-            )
+            nc.vector.scalar_tensor_tensor(by_cos[k][:], p_ps[k][:], b_plain[:, k : k + 1], cos_sb[k][:], ADD, MULT)
+            nc.vector.scalar_tensor_tensor(by_sin[k][:], r_ps[k][:], b_turned[:, k : k + 1], sin_sb[k][:], ADD, MULT)
         for k in range(BLOCKS):
             turned = held.tile([P, TOKENS], F32, name=f"turned{k}")
             nc.vector.tensor_add(turned[:], by_cos[k][:], by_sin[k][:])

@@ -4,12 +4,28 @@ P = 128
 WORDS = 1024
 FEATS = 256
 TOKENS = 256
-HALF = 32
-BLOCKS = FEATS // P
+PLACES = 32
+HEADS = FEATS // (2 * PLACES)
+LOW, HIGH = 0, 1
 FLOPS = 2 * P * FEATS * TOKENS
 
 BF16, F32, U16 = mybir.dt.bfloat16, mybir.dt.float32, mybir.dt.uint16
 ADD, MULT = mybir.AluOpType.add, mybir.AluOpType.mult
+
+
+def dram_by_head(dram):
+    return dram.rearrange("(h t q) j -> h q t j", t=2, q=PLACES)
+
+
+def tile_by_head(tile_ap):
+    return tile_ap.rearrange("(q h) t j -> h q t j", h=HEADS)
+
+
+def sort_columns(nc, dst, src, t):
+    nc.vector.tensor_copy(
+        dst.rearrange("r (q h) -> r q h", h=HEADS),
+        src.rearrange("r (h t q) -> r t q h", t=2, q=PLACES)[:, t],
+    )
 
 
 def tile_molformer_kernel(tc, table, w, b, cos_t, sin_t, offs, out):
@@ -18,51 +34,52 @@ def tile_molformer_kernel(tc, table, w, b, cos_t, sin_t, offs, out):
         tc.tile_pool(name="held", bufs=1) as held,
         tc.psum_pool(name="psum", bufs=1) as psum,
     ):
+        queue_of_head = [nc.scalar if h % 2 == 0 else nc.sync for h in range(HEADS)]
+        cos_sb = held.tile([P, 2, TOKENS], F32, name="cos_sb")
+        sin_sb = held.tile([P, 2, TOKENS], F32, name="sin_sb")
+        b_row = held.tile([1, FEATS], F32, name="b_row")
+        nc.scalar.dma_start(b_row[:], b.rearrange("m o -> o m"))
         offsets = held.tile([P, TOKENS // 16], U16, name="offsets")
         nc.sync.dma_start(offsets[:], offs)
         w_plain = held.tile([P, FEATS], BF16, name="w_plain")
         nc.scalar.dma_start(w_plain[:], w)
+        queue_of_head[0].dma_start(tile_by_head(cos_sb[:])[0], dram_by_head(cos_t)[0])
         words = held.tile([P, WORDS], BF16, name="words")
         nc.sync.dma_start(words[:], table)
+        for h in range(1, HEADS):
+            queue_of_head[h].dma_start(tile_by_head(cos_sb[:])[h], dram_by_head(cos_t)[h])
+        for h in range(HEADS):
+            queue_of_head[h].dma_start(tile_by_head(sin_sb[:])[h], dram_by_head(sin_t)[h])
 
-        b_cols = b.rearrange("(k p) o -> p (k o)", p=P)
-        b_plain = held.tile([P, BLOCKS], F32, name="b_plain")
-        b_turned = held.tile([P, BLOCKS], F32, name="b_turned")
-        with nc.allow_non_contiguous_dma(reason="a bias of 256 values, one value to a partition"):
-            nc.scalar.dma_start(b_plain[:], b_cols)
-            for first in range(0, P, 2 * HALF):
-                second = first + HALF
-                nc.sync.dma_start(b_turned[first : first + HALF, :], b_cols[second : second + HALF, :])
-                nc.scalar.dma_start(b_turned[second : second + HALF, :], b_cols[first : first + HALF, :])
+        b_half = [held.tile([1, P], F32, name=f"b_half{t}") for t in (LOW, HIGH)]
+        w_half = [held.tile([P, P], BF16, name=f"w_half{t}") for t in (LOW, HIGH)]
+        for t in (LOW, HIGH):
+            sort_columns(nc, b_half[t][:], b_row[:], t)
+        for t in (LOW, HIGH):
+            sort_columns(nc, w_half[t][:], w_plain[:], t)
 
-        cos_sb = [held.tile([P, TOKENS], F32, name=f"cos{k}") for k in range(BLOCKS)]
-        sin_sb = [held.tile([P, TOKENS], F32, name=f"sin{k}") for k in range(BLOCKS)]
-        for k in range(BLOCKS):
-            nc.scalar.dma_start(cos_sb[k][:], cos_t[k * P : (k + 1) * P, :])
-            nc.sync.dma_start(sin_sb[k][:], sin_t[k * P : (k + 1) * P, :])
+        one = held.tile([1, 1], F32, name="one")
+        nc.vector.memset(one[:], 1.0)
+        bias_ps = psum.tile([P, 2], F32, name="bias_ps")
+        for t in (LOW, HIGH):
+            nc.tensor.matmul(bias_ps[:, t : t + 1], b_half[t][:], one[:])
+        bias = held.tile([P, 2], F32, name="bias")
+        nc.vector.tensor_copy(bias[:], bias_ps[:])
 
-        w_turned = held.tile([P, FEATS], BF16, name="w_turned")
-        to = w_turned[:].rearrange("d (h t q) -> d h t q", t=2, q=HALF)
-        frm = w_plain[:].rearrange("d (h t q) -> d h t q", t=2, q=HALF)
-        nc.vector.tensor_scalar_mul(to[:, :, 0, :], frm[:, :, 1, :], -1.0)
-        nc.vector.tensor_copy(to[:, :, 1, :], frm[:, :, 0, :])
-        for first in range(0, P, 2 * HALF):
-            nc.gpsimd.tensor_scalar_mul(b_turned[first : first + HALF, :], b_turned[first : first + HALF, :], -1.0)
+        p_ps = [psum.tile([P, TOKENS], F32, name=f"p_ps{t}") for t in (LOW, HIGH)]
+        for t in (LOW, HIGH):
+            nc.tensor.matmul(p_ps[t][:], w_half[t][:], words[:].indirect(offsets[:]))
 
-        p_ps = [psum.tile([P, TOKENS], F32, name=f"p_ps{k}") for k in range(BLOCKS)]
-        r_ps = [psum.tile([P, TOKENS], F32, name=f"r_ps{k}") for k in range(BLOCKS)]
-        for k in range(BLOCKS):
-            block = slice(k * P, (k + 1) * P)
-            nc.tensor.matmul(p_ps[k][:], w_plain[:, block], words[:].indirect(offsets[:]))
-            nc.tensor.matmul(r_ps[k][:], w_turned[:, block], words[:].indirect(offsets[:]))
-
-        by_cos = [held.tile([P, TOKENS], F32, name=f"by_cos{k}") for k in range(BLOCKS)]
-        by_sin = [held.tile([P, TOKENS], F32, name=f"by_sin{k}") for k in range(BLOCKS)]
-        for k in range(BLOCKS):
-            nc.vector.scalar_tensor_tensor(by_cos[k][:], p_ps[k][:], b_plain[:, k : k + 1], cos_sb[k][:], ADD, MULT)
-            nc.vector.scalar_tensor_tensor(by_sin[k][:], r_ps[k][:], b_turned[:, k : k + 1], sin_sb[k][:], ADD, MULT)
-        for k in range(BLOCKS):
-            turned = held.tile([P, TOKENS], F32, name=f"turned{k}")
-            nc.vector.tensor_add(turned[:], by_cos[k][:], by_sin[k][:])
-            queue = nc.sync if k % 2 == 0 else nc.scalar
-            queue.dma_start(out[k * P : (k + 1) * P, :], turned[:])
+        by_cos = held.tile([P, 2, TOKENS], F32, name="by_cos")
+        by_sin = held.tile([P, 2, TOKENS], F32, name="by_sin")
+        for t in (LOW, HIGH):
+            nc.vector.scalar_tensor_tensor(by_cos[:, t, :], p_ps[t][:], bias[:, t : t + 1], cos_sb[:, t, :], ADD, MULT)
+        for t in (LOW, HIGH):
+            nc.vector.scalar_tensor_tensor(by_sin[:, t, :], p_ps[t][:], bias[:, t : t + 1], sin_sb[:, 1 - t, :], ADD, MULT)
+        out_sb = held.tile([P, 2, TOKENS], F32, name="out_sb")
+        nc.vector.tensor_sub(out_sb[:, LOW, :], by_cos[:, LOW, :], by_sin[:, HIGH, :])
+        for h in range(HEADS):
+            queue_of_head[h].dma_start(dram_by_head(out)[h][:, LOW, :], tile_by_head(out_sb[:])[h][:, LOW, :])
+        nc.vector.tensor_add(out_sb[:, HIGH, :], by_cos[:, HIGH, :], by_sin[:, LOW, :])
+        for h in range(HEADS):
+            queue_of_head[h].dma_start(dram_by_head(out)[h][:, HIGH, :], tile_by_head(out_sb[:])[h][:, HIGH, :])

@@ -60,11 +60,9 @@ def tile_molformer_kernel(tc, table, w, b, cos_t, sin_t, offs, out):
 
         one = held.tile([1, 1], F32, name="one")
         nc.vector.memset(one[:], 1.0)
-        bias_ps = psum.tile([P, 2], F32, name="bias_ps")
+        bias = psum.tile([P, 2], F32, name="bias")
         for t in (LOW, HIGH):
-            nc.tensor.matmul(bias_ps[:, t : t + 1], b_half[t][:], one[:])
-        bias = held.tile([P, 2], F32, name="bias")
-        nc.vector.tensor_copy(bias[:], bias_ps[:])
+            nc.tensor.matmul(bias[:, t : t + 1], b_half[t][:], one[:])
 
         p_ps = [psum.tile([P, TOKENS], F32, name=f"p_ps{t}") for t in (LOW, HIGH)]
         for t in (LOW, HIGH):
@@ -75,7 +73,10 @@ def tile_molformer_kernel(tc, table, w, b, cos_t, sin_t, offs, out):
         for t in (LOW, HIGH):
             nc.vector.scalar_tensor_tensor(by_cos[:, t, :], p_ps[t][:], bias[:, t : t + 1], cos_sb[:, t, :], ADD, MULT)
         for t in (LOW, HIGH):
-            nc.vector.scalar_tensor_tensor(by_sin[:, t, :], p_ps[t][:], bias[:, t : t + 1], sin_sb[:, 1 - t, :], ADD, MULT)
+            other = 1 - t
+            nc.vector.scalar_tensor_tensor(
+                by_sin[:, t, :], p_ps[t][:], bias[:, t : t + 1], sin_sb[:, other, :], ADD, MULT
+            )
         out_sb = held.tile([P, 2, TOKENS], F32, name="out_sb")
         nc.vector.tensor_sub(out_sb[:, LOW, :], by_cos[:, LOW, :], by_sin[:, HIGH, :])
         for h in range(HEADS):

@@ -13,12 +13,8 @@ BF16, F32, U16 = mybir.dt.bfloat16, mybir.dt.float32, mybir.dt.uint16
 ADD, MULT = mybir.AluOpType.add, mybir.AluOpType.mult
 
 
-def dram_by_head(dram):
-    return dram.rearrange("(h t q) j -> h q t j", t=2, q=PLACES)
-
-
-def tile_by_head(tile_ap):
-    return tile_ap.rearrange("(q h) t j -> h q t j", h=HEADS)
+def dram_half(dram, t):
+    return dram.rearrange("(h t q) j -> t q h j", t=2, q=PLACES)[t]
 
 
 def sort_columns(nc, dst, src, t):
@@ -34,7 +30,6 @@ def tile_molformer_kernel(tc, table, w, b, cos_t, sin_t, offs, out):
         tc.tile_pool(name="held", bufs=1) as held,
         tc.psum_pool(name="psum", bufs=1) as psum,
     ):
-        queue_of_head = [nc.scalar if h % 2 == 0 else nc.sync for h in range(HEADS)]
         cos_sb = held.tile([P, 2, TOKENS], F32, name="cos_sb")
         sin_sb = held.tile([P, 2, TOKENS], F32, name="sin_sb")
         b_row = held.tile([1, FEATS], F32, name="b_row")
@@ -43,13 +38,12 @@ def tile_molformer_kernel(tc, table, w, b, cos_t, sin_t, offs, out):
         nc.sync.dma_start(offsets[:], offs)
         w_plain = held.tile([P, FEATS], BF16, name="w_plain")
         nc.scalar.dma_start(w_plain[:], w)
-        queue_of_head[0].dma_start(tile_by_head(cos_sb[:])[0], dram_by_head(cos_t)[0])
         words = held.tile([P, WORDS], BF16, name="words")
         nc.sync.dma_start(words[:], table)
-        for h in range(1, HEADS):
-            queue_of_head[h].dma_start(tile_by_head(cos_sb[:])[h], dram_by_head(cos_t)[h])
-        for h in range(HEADS):
-            queue_of_head[h].dma_start(tile_by_head(sin_sb[:])[h], dram_by_head(sin_t)[h])
+        nc.scalar.dma_start(cos_sb[:, LOW, :], dram_half(cos_t, LOW))
+        nc.sync.dma_start(cos_sb[:, HIGH, :], dram_half(cos_t, HIGH))
+        nc.scalar.dma_start(sin_sb[:, HIGH, :], dram_half(sin_t, HIGH))
+        nc.sync.dma_start(sin_sb[:, LOW, :], dram_half(sin_t, LOW))
 
         b_half = [held.tile([1, P], F32, name=f"b_half{t}") for t in (LOW, HIGH)]
         w_half = [held.tile([P, P], BF16, name=f"w_half{t}") for t in (LOW, HIGH)]
@@ -79,8 +73,6 @@ def tile_molformer_kernel(tc, table, w, b, cos_t, sin_t, offs, out):
             )
         out_sb = held.tile([P, 2, TOKENS], F32, name="out_sb")
         nc.vector.tensor_sub(out_sb[:, LOW, :], by_cos[:, LOW, :], by_sin[:, HIGH, :])
-        for h in range(HEADS):
-            queue_of_head[h].dma_start(dram_by_head(out)[h][:, LOW, :], tile_by_head(out_sb[:])[h][:, LOW, :])
+        nc.sync.dma_start(dram_half(out, LOW), out_sb[:, LOW, :])
         nc.vector.tensor_add(out_sb[:, HIGH, :], by_cos[:, HIGH, :], by_sin[:, LOW, :])
-        for h in range(HEADS):
-            queue_of_head[h].dma_start(dram_by_head(out)[h][:, HIGH, :], tile_by_head(out_sb[:])[h][:, HIGH, :])
+        nc.scalar.dma_start(dram_half(out, HIGH), out_sb[:, HIGH, :])

@@ -65,14 +65,13 @@ def tile_molformer_kernel(tc, table, w, b, cos_t, sin_t, offs, out):
         by_cos = held.tile([P, 2, TOKENS], F32, name="by_cos")
         by_sin = held.tile([P, 2, TOKENS], F32, name="by_sin")
         for t in (LOW, HIGH):
-            nc.vector.scalar_tensor_tensor(by_cos[:, t, :], p_ps[t][:], bias[:, t : t + 1], cos_sb[:, t, :], ADD, MULT)
-        for t in (LOW, HIGH):
             other = 1 - t
+            nc.vector.scalar_tensor_tensor(by_cos[:, t, :], p_ps[t][:], bias[:, t : t + 1], cos_sb[:, t, :], ADD, MULT)
             nc.vector.scalar_tensor_tensor(
                 by_sin[:, t, :], p_ps[t][:], bias[:, t : t + 1], sin_sb[:, other, :], ADD, MULT
             )
         out_sb = held.tile([P, 2, TOKENS], F32, name="out_sb")
-        nc.vector.tensor_sub(out_sb[:, LOW, :], by_cos[:, LOW, :], by_sin[:, HIGH, :])
-        nc.sync.dma_start(dram_half(out, LOW), out_sb[:, LOW, :])
         nc.vector.tensor_add(out_sb[:, HIGH, :], by_cos[:, HIGH, :], by_sin[:, LOW, :])
         nc.scalar.dma_start(dram_half(out, HIGH), out_sb[:, HIGH, :])
+        nc.vector.tensor_sub(out_sb[:, LOW, :], by_cos[:, LOW, :], by_sin[:, HIGH, :])
+        nc.sync.dma_start(dram_half(out, LOW), out_sb[:, LOW, :])

@@ -73,5 +73,7 @@ def tile_molformer_kernel(tc, table, w, b, cos_t, sin_t, offs, out):
         out_sb = held.tile([P, 2, TOKENS], F32, name="out_sb")
         nc.vector.tensor_add(out_sb[:, HIGH, :], by_cos[:, HIGH, :], by_sin[:, LOW, :])
         nc.scalar.dma_start(dram_half(out, HIGH), out_sb[:, HIGH, :])
-        nc.vector.tensor_sub(out_sb[:, LOW, :], by_cos[:, LOW, :], by_sin[:, HIGH, :])
-        nc.sync.dma_start(dram_half(out, LOW), out_sb[:, LOW, :])
+        for first in range(0, TOKENS, TOKENS // 2):
+            piece = slice(first, first + TOKENS // 2)
+            nc.vector.tensor_sub(out_sb[:, LOW, piece], by_cos[:, LOW, piece], by_sin[:, HIGH, piece])
+            nc.sync.dma_start(dram_half(out, LOW)[:, :, piece], out_sb[:, LOW, piece])

import concourse.mybir as mybir

P = 128
WORDS = 1024
FEATS = 256
TOKENS = 256
PLACES = 32
HEADS = FEATS // (2 * PLACES)
LOW, HIGH = 0, 1
FLOPS = 2 * P * FEATS * TOKENS

BF16, F32, U16 = mybir.dt.bfloat16, mybir.dt.float32, mybir.dt.uint16
ADD, MULT = mybir.AluOpType.add, mybir.AluOpType.mult


def dram_half(dram, t):
    return dram.rearrange("(h t q) j -> t q h j", t=2, q=PLACES)[t]


def sort_columns(nc, dst, src, t):
    nc.vector.tensor_copy(
        dst.rearrange("r (q h) -> r q h", h=HEADS),
        src.rearrange("r (h t q) -> r t q h", t=2, q=PLACES)[:, t],
    )


def tile_molformer_kernel(tc, table, w, b, cos_t, sin_t, offs, out):
    nc = tc.nc
    with (
        tc.tile_pool(name="held", bufs=1) as held,
        tc.psum_pool(name="psum", bufs=1) as psum,
    ):
        cos_sb = held.tile([P, 2, TOKENS], F32, name="cos_sb")
        sin_sb = held.tile([P, 2, TOKENS], F32, name="sin_sb")
        b_row = held.tile([1, FEATS], F32, name="b_row")
        nc.scalar.dma_start(b_row[:], b.rearrange("m o -> o m"))
        offsets = held.tile([P, TOKENS // 16], U16, name="offsets")
        nc.sync.dma_start(offsets[:], offs)
        w_plain = held.tile([P, FEATS], BF16, name="w_plain")
        nc.scalar.dma_start(w_plain[:], w)
        words = held.tile([P, WORDS], BF16, name="words")
        nc.sync.dma_start(words[:], table)
        nc.scalar.dma_start(cos_sb[:, LOW, :], dram_half(cos_t, LOW))
        nc.sync.dma_start(cos_sb[:, HIGH, :], dram_half(cos_t, HIGH))
        nc.scalar.dma_start(sin_sb[:, HIGH, :], dram_half(sin_t, HIGH))
        nc.sync.dma_start(sin_sb[:, LOW, :], dram_half(sin_t, LOW))

        b_half = [held.tile([1, P], F32, name=f"b_half{t}") for t in (LOW, HIGH)]
        w_half = [held.tile([P, P], BF16, name=f"w_half{t}") for t in (LOW, HIGH)]
        for t in (LOW, HIGH):
            sort_columns(nc, b_half[t][:], b_row[:], t)
        for t in (LOW, HIGH):
            sort_columns(nc, w_half[t][:], w_plain[:], t)

        one = held.tile([1, 1], F32, name="one")
        nc.vector.memset(one[:], 1.0)
        bias = psum.tile([P, 2], F32, name="bias")
        for t in (LOW, HIGH):
            nc.tensor.matmul(bias[:, t : t + 1], b_half[t][:], one[:])

        p_ps = [psum.tile([P, TOKENS], F32, name=f"p_ps{t}") for t in (LOW, HIGH)]
        for t in (LOW, HIGH):
            nc.tensor.matmul(p_ps[t][:], w_half[t][:], words[:].indirect(offsets[:]))

        by_cos = held.tile([P, 2, TOKENS], F32, name="by_cos")
        by_sin = held.tile([P, 2, TOKENS], F32, name="by_sin")
        for t in (LOW, HIGH):
            other = 1 - t
            nc.vector.scalar_tensor_tensor(by_cos[:, t, :], p_ps[t][:], bias[:, t : t + 1], cos_sb[:, t, :], ADD, MULT)
            nc.vector.scalar_tensor_tensor(
                by_sin[:, t, :], p_ps[t][:], bias[:, t : t + 1], sin_sb[:, other, :], ADD, MULT
            )
        out_sb = held.tile([P, 2, TOKENS], F32, name="out_sb")
        nc.vector.tensor_add(out_sb[:, HIGH, :], by_cos[:, HIGH, :], by_sin[:, LOW, :])
        nc.scalar.dma_start(dram_half(out, HIGH), out_sb[:, HIGH, :])
        for first in range(0, TOKENS, TOKENS // 2):
            piece = slice(first, first + TOKENS // 2)
            nc.vector.tensor_sub(out_sb[:, LOW, piece], by_cos[:, LOW, piece], by_sin[:, HIGH, piece])
            nc.sync.dma_start(dram_half(out, LOW)[:, :, piece], out_sb[:, LOW, piece])
